import numpy as np
import ml_dtypes


def mxq(x, axis, fmt="e4m3"):
    dtype, down = {"e4m3": (ml_dtypes.float8_e4m3fn, 7), "e5m2": (ml_dtypes.float8_e5m2, 14)}[fmt]
    v = np.moveaxis(np.asarray(x, np.float32).astype(ml_dtypes.bfloat16).astype(np.float64), axis, -1)
    blocks = v.reshape(v.shape[:-1] + (-1, 32))
    amax = np.abs(blocks).max(-1, keepdims=True)
    byte = np.maximum(np.where(amax > 0, np.frexp(amax)[1] - 1 + 127, 0) - down, 1)
    scale = np.exp2(byte - 127.0)
    codes = (blocks / scale).astype(np.float32).astype(dtype).astype(np.float64)
    return np.moveaxis((codes * scale).reshape(v.shape), -1, axis)


WIDE = False


def mx_kscale(k):
    if not WIDE:
        return np.ones(k)
    levels = np.array([10, -10, 5, -5, 0])
    a = np.random.permutation(np.resize(levels, k // 512 * 4)).reshape(k // 512, 4)
    idx = np.arange(k)
    return np.exp2(a[idx // 512, idx % 128 // 32])


BF16 = ml_dtypes.bfloat16


def bf(x):
    return np.asarray(x, np.float32).astype(BF16)


def f64(x):
    return np.asarray(x).astype(np.float64)


B, N, D, DK, DV, HQ, WQ, HS, WS = 16, 8, 512, 512, 128, 16, 16, 8, 16
U = HQ * WQ
V = HS * WS
VS = 4.0 * np.sqrt(N) / U


def setup_inputs():
    s = mx_kscale(D)
    sc = s[None, :, None, None]
    offset = np.random.standard_normal((B, D))[:, :, None, None]
    return {"query": bf((np.random.standard_normal((B, D, HQ, WQ)) + offset) * sc),
            "support": bf(np.random.standard_normal((N, D, HS, WS)) * sc),
            "Wk": bf(np.random.standard_normal((DK, D)) / np.sqrt(D) / s[None, :]),
            "Wv": bf(np.random.standard_normal((DV, D)) * VS / np.sqrt(D) / s[None, :])}


def reference(query, support, Wk, Wv):
    qf = mxq(f64(query).reshape(B, D, U), 1, "e4m3")
    sf = mxq(f64(support).reshape(N, D, V), 1, "e4m3")
    wk = mxq(f64(Wk), 1, "e4m3")
    wv = mxq(f64(Wv), 1, "e4m3")
    q = wk @ qf
    support_key = wk @ sf
    support_value = wv @ sf
    scores = (mxq(q, 1, "e4m3").transpose(0, 2, 1)[:, None] @ mxq(support_key, 1, "e4m3")[None]) / np.sqrt(DK)
    e = np.exp(scores - scores.max(1, keepdims=True))
    attn = e / e.sum(1, keepdims=True)
    return (attn.sum(2)[:, :, None, :] * support_value[None]).sum(1)

@@ -1,0 +1,349 @@
+import math
+from contextlib import ExitStack
+
+import concourse.mybir as mybir
+from concourse.masks import make_identity
+
+F32 = mybir.dt.float32
+BF16 = mybir.dt.bfloat16
+U32 = mybir.dt.uint32
+U8 = mybir.dt.uint8
+FP8X4 = mybir.dt.float8_e4m3fn_x4
+ACT = mybir.ActivationFunctionType
+ALU = mybir.AluOpType
+
+P = 128
+PACK = 4
+B, N_SUP, D, DK, DV, U, V = 16, 8, 512, 512, 128, 256, 128
+PAIR = 2
+N_PAIRS = B // PAIR
+FIRST_ROUNDS = 3
+STORE = 4
+GROUP = 4
+SUM_LAG = GROUP + 1
+RUN = 4
+
+FLOPS = 2 * (B * DK * D * U + N_SUP * DK * D * V + N_SUP * DV * D * V + B * N_SUP * U * V * DK)
+
+
+def tile_crossattention_pa_t_kernel(tc, query, support, Wk, Wv, out):
+    nc = tc.nc
+    with ExitStack() as ctx:
+        keep = ctx.enter_context(tc.tile_pool(name="keep", bufs=1))
+        rows_pool = ctx.enter_context(tc.tile_pool(name="rows", bufs=N_PAIRS))
+        stage = ctx.enter_context(tc.tile_pool(name="stage", bufs=2))
+        soft = ctx.enter_context(tc.tile_pool(name="soft", bufs=2))
+        exp_pool = ctx.enter_context(tc.tile_pool(name="exp_pool", bufs=GROUP + 2))
+        score_psum = ctx.enter_context(tc.psum_pool(name="score_psum", bufs=4))
+        turn_psum = ctx.enter_context(tc.psum_pool(name="turn_psum", bufs=3))
+        result_psum = ctx.enter_context(tc.psum_pool(name="result_psum", bufs=1))
+
+        wk_rows = keep.tile([P, PACK * D], BF16)
+        nc.sync.dma_start(out=wk_rows[:], in_=Wk.rearrange("(p t) d -> p (t d)", t=PACK))
+        wv_rows = keep.tile([P, D], BF16)
+        nc.sync.dma_start(out=wv_rows[:], in_=Wv)
+        sup_rows = keep.tile([P, N_SUP, PACK * V], BF16)
+        nc.sync.dma_start(
+            out=sup_rows[:], in_=support.rearrange("n (p j) h w -> p n (j h w)", j=PACK)
+        )
+        query_rows = []
+        for g in range(N_PAIRS):
+            q_rows = rows_pool.tile([P, PAIR, PACK * U], BF16)
+            nc.sync.dma_start(
+                out=q_rows[:],
+                in_=query[g * PAIR : (g + 1) * PAIR].rearrange(
+                    "b (p j) h w -> p b (j h w)", j=PACK
+                ),
+            )
+            query_rows.append(q_rows)
+
+        ident = keep.tile([P, P], F32)
+        make_identity(nc, ident[:])
+
+        def regroup(engine_copy, grouped, rows):
+            engine_copy(
+                out=grouped.rearrange("p (c r j) -> p c j r", r=RUN, j=PACK),
+                in_=rows.rearrange("p (j c r) -> p c j r", j=PACK, r=RUN),
+            )
+
+        def quantise(codes, scales, grouped):
+            nc.vector.quantize_mx(out=codes.bitcast(FP8X4), scales=scales, in_=grouped)
+
+        def weight_to_codes(rows, n_chunks, grouped, codes, scales):
+            words = rows.bitcast(F32).rearrange("p (t w e) -> p t e w", t=n_chunks, e=2)
+            grouped_words = grouped.bitcast(F32).rearrange("p (t k e) -> p t k e", t=n_chunks, e=2)
+            for t in range(n_chunks):
+                planes = score_psum.tile([P, 2, P], F32, tag="bank")
+                for e in range(2):
+                    nc.tensor.transpose(planes[:, e, :], words[:, t, e, :], ident[:])
+                nc.vector.tensor_copy(
+                    out=grouped_words[:, t], in_=planes[:].rearrange("p e k -> p k e")
+                )
+            quantise(codes, scales, grouped)
+
+        def project_with_wk(psum, tag, x_codes, x_scales, grouped, n_blocks, copies):
+            for blk in range(n_blocks):
+                cols = slice(blk * P, (blk + 1) * P)
+                prod = psum.tile([P, PACK, P], F32, tag=tag)
+                for j in range(PACK):
+                    chunk = slice(j * P, (j + 1) * P)
+                    nc.tensor.matmul_mx(
+                        out=prod[:, j, :],
+                        lhsT=wk_codes[:, chunk].bitcast(FP8X4),
+                        lhsT_scale=wk_scales[:, chunk],
+                        rhs=x_codes[:, cols].bitcast(FP8X4),
+                        rhs_scale=x_scales[:, cols],
+                        start=True,
+                        stop=True,
+                    )
+                copies[blk % len(copies)](
+                    out=grouped[:, blk * P * PACK : (blk + 1) * P * PACK].rearrange(
+                        "p (c j) -> p c j", j=PACK
+                    ),
+                    in_=prod[:].rearrange("p j c -> p c j"),
+                )
+
+        pair_width = PAIR * U
+        qf_grouped, qf_operands, q_grouped = {}, {}, {}
+        q_codes = keep.tile([P, B * U], U32, align_bytes=64)
+        q_scales = keep.tile([P, B * U], U8, align_bytes=64)
+
+        def regroup_queries(g):
+            grouped = stage.tile([P, pair_width * PACK], BF16, align_bytes=64, tag="qf_grouped")
+            for i in range(PAIR):
+                regroup(
+                    nc.vector.tensor_copy,
+                    grouped[:, i * U * PACK : (i + 1) * U * PACK],
+                    query_rows[g][:, i, :],
+                )
+            qf_grouped[g] = grouped
+
+        def quantise_queries(g):
+            codes = stage.tile([P, pair_width], U32, align_bytes=64, tag="qf_codes")
+            scales = stage.tile([P, pair_width], U8, align_bytes=64, tag="qf_scales")
+            quantise(codes[:], scales[:], qf_grouped[g][:])
+            qf_operands[g] = (codes, scales)
+
+        def project_queries(g):
+            grouped = stage.tile([P, pair_width * PACK], BF16, align_bytes=64, tag="q_grouped")
+            codes, scales = qf_operands[g]
+            project_with_wk(
+                turn_psum, "turn", codes, scales, grouped, pair_width // P, [nc.scalar.copy]
+            )
+            q_grouped[g] = grouped
+
+        def quantise_projected(g):
+            cols = slice(g * pair_width, (g + 1) * pair_width)
+            quantise(q_codes[:, cols], q_scales[:, cols], q_grouped[g][:])
+
+        score_banks, exps, denoms, recips, turned, weights, products, results = (
+            {}, {}, {}, {}, {}, {}, {}, {}
+        )
+
+        def scores(b, half):
+            u_cols = slice(b * U + half * P, b * U + (half + 1) * P)
+            banks = []
+            for j in range(2):
+                bank = score_psum.tile([P, N_SUP // 2, P], F32, tag="bank")
+                for i in range(N_SUP // 2):
+                    n = j * (N_SUP // 2) + i
+                    v_cols = slice(n * V, (n + 1) * V)
+                    nc.tensor.matmul_mx(
+                        out=bank[:, i, :],
+                        lhsT=key_codes[:, v_cols].bitcast(FP8X4),
+                        lhsT_scale=key_scales[:, v_cols],
+                        rhs=q_codes[:, u_cols].bitcast(FP8X4),
+                        rhs_scale=q_scales[:, u_cols],
+                        start=True,
+                        stop=True,
+                    )
+                banks.append(bank)
+            low = soft.tile([P, N_SUP // 2, P], F32, bufs=3)
+            nc.scalar.copy(out=low[:], in_=banks[0][:])
+            score_banks[b, half] = (low, banks[1])
+
+        def shift_and_exp(b, half):
+            if half == 0:
+                expd = exp_pool.tile([P, N_SUP, U], F32)
+                exps[b] = expd
+            low, high = score_banks[b, half]
+            top4 = soft.tile([P, N_SUP // 2, P], F32)
+            nc.vector.tensor_max(out=top4[:], in0=high[:], in1=low[:])
+            top2 = soft.tile([P, 2, P], F32)
+            nc.vector.tensor_max(out=top2[:], in0=top4[:, 0:2, :], in1=top4[:, 2:4, :])
+            top = soft.tile([P, P], F32)
+            nc.vector.tensor_max(out=top[:], in0=top2[:, 0, :], in1=top2[:, 1, :])
+            mine = exps[b][:, :, half * P : (half + 1) * P]
+            top_of_each = top[:].unsqueeze(1).to_broadcast([P, N_SUP // 2, P])
+            nc.gpsimd.tensor_tensor(
+                out=mine[:, 0 : N_SUP // 2, :], in0=low[:], in1=top_of_each, op=ALU.subtract
+            )
+            nc.vector.tensor_sub(out=mine[:, N_SUP // 2 : N_SUP, :], in0=high[:], in1=top_of_each)
+            nc.scalar.activation(out=mine, in_=mine, func=ACT.Exp, scale=1.0 / math.sqrt(DK))
+
+        def add_transposed(out_ps, terms):
+            for i, term in enumerate(terms):
+                nc.tensor.matmul(
+                    out=out_ps,
+                    lhsT=term,
+                    rhs=ident[:],
+                    is_transpose=True,
+                    start=(i == 0),
+                    stop=(i == len(terms) - 1),
+                )
+
+        def add_over_n(b):
+            if b % GROUP == 0:
+                denom = soft.tile([P, GROUP, U // P, V], F32)
+                denoms[b // GROUP] = denom
+            denom_ps = turn_psum.tile([P, U // P, V], F32, tag="turn")
+            for half in range(U // P):
+                add_transposed(
+                    denom_ps[:, half, :],
+                    [exps[b][:, n, half * P : (half + 1) * P] for n in range(N_SUP)],
+                )
+            nc.scalar.copy(out=denoms[b // GROUP][:, b % GROUP], in_=denom_ps[:])
+
+        def invert(group):
+            logs = soft.tile([P, GROUP, U // P, V], F32)
+            nc.scalar.activation(out=logs[:], in_=denoms[group][:], func=ACT.Ln)
+            recip = soft.tile([P, GROUP, U // P, V], F32)
+            nc.scalar.activation(out=recip[:], in_=logs[:], func=ACT.Exp, scale=-1.0)
+            recips[group] = recip
+
+        def turn_back(b):
+            recip_ps = turn_psum.tile([P, U], F32, tag="turn")
+            for half in range(U // P):
+                nc.tensor.transpose(
+                    recip_ps[:, half * P : (half + 1) * P],
+                    recips[b // GROUP][:, b % GROUP, half, :],
+                    ident[:],
+                )
+            turned[b] = recip_ps
+
+        def sum_softmax(b):
+            attn = soft.tile([P, N_SUP, U], F32, bufs=1)
+            weight = soft.tile([P, N_SUP], F32)
+            for n in range(N_SUP):
+                nc.vector.scalar_tensor_tensor(
+                    out=attn[:, n, :],
+                    in0=exps[b][:, n, :],
+                    scalar=1.0,
+                    in1=turned[b][:],
+                    op0=ALU.mult,
+                    op1=ALU.mult,
+                    accum_out=weight[:, n : n + 1],
+                )
+            weights[b] = weight
+
+        def weigh_values(b):
+            weighted = soft.tile([P, N_SUP, DV], F32)
+            nc.gpsimd.tensor_tensor(
+                out=weighted[:],
+                in0=val_t[:],
+                in1=weights[b][:].unsqueeze(2).to_broadcast([P, N_SUP, DV]),
+                op=ALU.mult,
+            )
+            products[b] = weighted
+
+        def combine(b):
+            if b % STORE == 0:
+                result_ps = result_psum.tile([P, STORE, V], F32)
+                results[b // STORE] = result_ps
+            add_transposed(
+                results[b // STORE][:, b % STORE, :], [products[b][:, n, :] for n in range(N_SUP)]
+            )
+
+        def store_results(last):
+            result_sb = soft.tile([P, STORE, V], F32)
+            nc.scalar.copy(out=result_sb[:], in_=results[last // STORE][:])
+            nc.sync.dma_start(
+                out=out[last - STORE + 1 : last + 1].rearrange("b c v -> c b v"), in_=result_sb[:]
+            )
+
+        wk_grouped = keep.tile([P, PACK * DK], BF16, align_bytes=64)
+        wk_codes = keep.tile([P, DK], U32, align_bytes=64)
+        wk_scales = keep.tile([P, DK], U8, align_bytes=64)
+        weight_to_codes(wk_rows[:], PACK, wk_grouped[:], wk_codes[:], wk_scales[:])
+        wv_grouped = keep.tile([P, PACK * DV], BF16, align_bytes=64)
+        wv_codes = keep.tile([P, DV], U32, align_bytes=64)
+        wv_scales = keep.tile([P, DV], U8, align_bytes=64)
+        weight_to_codes(wv_rows[:], 1, wv_grouped[:], wv_codes[:], wv_scales[:])
+
+
+        sup_grouped = keep.tile([P, N_SUP * V * PACK], BF16, align_bytes=64)
+        sup_codes = keep.tile([P, N_SUP * V], U32, align_bytes=64)
+        sup_scales = keep.tile([P, N_SUP * V], U8, align_bytes=64)
+        for n in range(N_SUP):
+            regroup(
+                nc.vector.tensor_copy,
+                sup_grouped[:, n * V * PACK : (n + 1) * V * PACK],
+                sup_rows[:, n, :],
+            )
+        quantise(sup_codes[:], sup_scales[:], sup_grouped[:])
+
+        key_grouped = keep.tile([P, N_SUP * V * PACK], BF16, align_bytes=64)
+        key_codes = keep.tile([P, N_SUP * V], U32, align_bytes=64)
+        key_scales = keep.tile([P, N_SUP * V], U8, align_bytes=64)
+        project_with_wk(
+            score_psum,
+            "bank",
+            sup_codes,
+            sup_scales,
+            key_grouped,
+            N_SUP,
+            [nc.scalar.copy, nc.vector.tensor_copy],
+        )
+        quantise(key_codes[:], key_scales[:], key_grouped[:])
+
+        val_t = keep.tile([P, N_SUP, DV], F32)
+        for half in range(N_SUP // PACK):
+            val_ps = score_psum.tile([P, PACK, DV], F32, tag="bank")
+            for i in range(PACK):
+                cols = slice((half * PACK + i) * V, (half * PACK + i + 1) * V)
+                nc.tensor.matmul_mx(
+                    out=val_ps[:, i, :],
+                    lhsT=sup_codes[:, cols].bitcast(FP8X4),
+                    lhsT_scale=sup_scales[:, cols],
+                    rhs=wv_codes[:].bitcast(FP8X4),
+                    rhs_scale=wv_scales[:],
+                    start=True,
+                    stop=True,
+                )
+            nc.scalar.copy(out=val_t[:, half * PACK : (half + 1) * PACK, :], in_=val_ps[:])
+
+        def projection_round(g):
+            if g < N_PAIRS:
+                regroup_queries(g)
+            if 0 <= g - 1 < N_PAIRS:
+                quantise_queries(g - 1)
+                project_queries(g - 1)
+            if 0 <= g - 2 < N_PAIRS:
+                quantise_projected(g - 2)
+
+        for g in range(FIRST_ROUNDS):
+            projection_round(g)
+
+        for half in range(U // P):
+            scores(0, half)
+        for k in range(B + SUM_LAG + 3):
+            if 0 <= k - SUM_LAG - 1 < B:
+                weigh_values(k - SUM_LAG - 1)
+            if 0 <= k - SUM_LAG - 3 and (k - SUM_LAG - 3) % STORE == STORE - 1:
+                store_results(k - SUM_LAG - 3)
+            for half in range(U // P):
+                if k < B:
+                    shift_and_exp(k, half)
+                if k + 1 < B:
+                    scores(k + 1, half)
+            if 0 <= k - 1 < B:
+                add_over_n(k - 1)
+                if k % GROUP == 0:
+                    invert((k - 1) // GROUP)
+            if 0 <= k - SUM_LAG - 2 < B:
+                combine(k - SUM_LAG - 2)
+            if 0 <= k - SUM_LAG < B:
+                sum_softmax(k - SUM_LAG)
+            if 0 <= k - SUM_LAG + 1 < B:
+                turn_back(k - SUM_LAG + 1)
+            projection_round(k + FIRST_ROUNDS)

@@ -21,6 +21,7 @@ FIRST_ROUNDS = 3
 STORE = 4
 GROUP = 4
 SUM_LAG = GROUP + 1
+N_FREE = N_SUP - 1
 RUN = 4
 
 FLOPS = 2 * (B * DK * D * U + N_SUP * DK * D * V + N_SUP * DV * D * V + B * N_SUP * U * V * DK)
@@ -169,10 +170,10 @@ def tile_crossattention_pa_t_kernel(tc, query, support, Wk, Wv, out):
             low, high = score_banks[b, half]
             top4 = soft.tile([P, N_SUP // 2, P], F32)
             nc.vector.tensor_max(out=top4[:], in0=high[:], in1=low[:])
-            top2 = soft.tile([P, 2, P], F32)
-            nc.vector.tensor_max(out=top2[:], in0=top4[:, 0:2, :], in1=top4[:, 2:4, :])
             top = soft.tile([P, P], F32)
-            nc.vector.tensor_max(out=top[:], in0=top2[:, 0, :], in1=top2[:, 1, :])
+            nc.vector.reduce_max(
+                out=top[:], in_=top4[:].rearrange("p n u -> p u n"), axis=mybir.AxisListType.X
+            )
             mine = exps[b][:, :, half * P : (half + 1) * P]
             top_of_each = top[:].unsqueeze(1).to_broadcast([P, N_SUP // 2, P])
             nc.gpsimd.tensor_tensor(
@@ -222,9 +223,9 @@ def tile_crossattention_pa_t_kernel(tc, query, support, Wk, Wv, out):
             turned[b] = recip_ps
 
         def sum_softmax(b):
-            attn = soft.tile([P, N_SUP, U], F32, bufs=1)
-            weight = soft.tile([P, N_SUP], F32)
-            for n in range(N_SUP):
+            attn = soft.tile([P, N_FREE, U], F32, bufs=1)
+            weight = soft.tile([P, N_FREE], F32)
+            for n in range(N_FREE):
                 nc.vector.scalar_tensor_tensor(
                     out=attn[:, n, :],
                     in0=exps[b][:, n, :],
@@ -237,11 +238,11 @@ def tile_crossattention_pa_t_kernel(tc, query, support, Wk, Wv, out):
             weights[b] = weight
 
         def weigh_values(b):
-            weighted = soft.tile([P, N_SUP, DV], F32)
+            weighted = soft.tile([P, N_FREE, DV], F32)
             nc.gpsimd.tensor_tensor(
                 out=weighted[:],
                 in0=val_t[:],
-                in1=weights[b][:].unsqueeze(2).to_broadcast([P, N_SUP, DV]),
+                in1=weights[b][:].unsqueeze(2).to_broadcast([P, N_FREE, DV]),
                 op=ALU.mult,
             )
             products[b] = weighted
@@ -251,7 +252,7 @@ def tile_crossattention_pa_t_kernel(tc, query, support, Wk, Wv, out):
                 result_ps = result_psum.tile([P, STORE, V], F32)
                 results[b // STORE] = result_ps
             add_transposed(
-                results[b // STORE][:, b % STORE, :], [products[b][:, n, :] for n in range(N_SUP)]
+                results[b // STORE][:, b % STORE, :], [products[b][:, n, :] for n in range(N_FREE)] + [base[:]]
             )
 
         def store_results(last):
@@ -296,8 +297,10 @@ def tile_crossattention_pa_t_kernel(tc, query, support, Wk, Wv, out):
         )
         quantise(key_codes[:], key_scales[:], key_grouped[:])
 
-        val_t = keep.tile([P, N_SUP, DV], F32)
-        for half in range(N_SUP // PACK):
+        val_t = keep.tile([P, N_FREE, DV], F32)
+        val_last = keep.tile([P, DV], F32)
+        base = keep.tile([P, DV], F32)
+        for half in reversed(range(N_SUP // PACK)):
             val_ps = score_psum.tile([P, PACK, DV], F32, tag="bank")
             for i in range(PACK):
                 cols = slice((half * PACK + i) * V, (half * PACK + i + 1) * V)
@@ -310,7 +313,15 @@ def tile_crossattention_pa_t_kernel(tc, query, support, Wk, Wv, out):
                     start=True,
                     stop=True,
                 )
-            nc.scalar.copy(out=val_t[:, half * PACK : (half + 1) * PACK, :], in_=val_ps[:])
+            if half == N_SUP // PACK - 1:
+                nc.scalar.copy(out=val_last[:], in_=val_ps[:, PACK - 1, :])
+                nc.scalar.mul(out=base[:], in_=val_last[:], mul=float(U))
+            n_here = min(N_FREE - half * PACK, PACK)
+            nc.vector.tensor_sub(
+                out=val_t[:, half * PACK : half * PACK + n_here, :],
+                in0=val_ps[:, 0:n_here, :],
+                in1=val_last[:].unsqueeze(1).to_broadcast([P, n_here, DV]),
+            )
 
         def projection_round(g):
             if g < N_PAIRS:

@@ -20,8 +20,10 @@ N_PAIRS = B // PAIR
 FIRST_ROUNDS = 3
 STORE = 4
 GROUP = 4
-SUM_LAG = GROUP + 1
+SUM_LAG = GROUP + 3
 N_FREE = N_SUP - 1
+SCALAR_SUP = 3
+SCALAR_PAIRS = 2
 RUN = 4
 
 FLOPS = 2 * (B * DK * D * U + N_SUP * DK * D * V + N_SUP * DV * D * V + B * N_SUP * U * V * DK)
@@ -33,8 +35,8 @@ def tile_crossattention_pa_t_kernel(tc, query, support, Wk, Wv, out):
         keep = ctx.enter_context(tc.tile_pool(name="keep", bufs=1))
         rows_pool = ctx.enter_context(tc.tile_pool(name="rows", bufs=N_PAIRS))
         stage = ctx.enter_context(tc.tile_pool(name="stage", bufs=2))
-        soft = ctx.enter_context(tc.tile_pool(name="soft", bufs=2))
-        exp_pool = ctx.enter_context(tc.tile_pool(name="exp_pool", bufs=GROUP + 2))
+        soft = ctx.enter_context(tc.tile_pool(name="soft", bufs=3))
+        exp_pool = ctx.enter_context(tc.tile_pool(name="exp_pool", bufs=GROUP + 4))
         score_psum = ctx.enter_context(tc.psum_pool(name="score_psum", bufs=4))
         turn_psum = ctx.enter_context(tc.psum_pool(name="turn_psum", bufs=3))
         result_psum = ctx.enter_context(tc.psum_pool(name="result_psum", bufs=1))
@@ -113,7 +115,7 @@ def tile_crossattention_pa_t_kernel(tc, query, support, Wk, Wv, out):
             grouped = stage.tile([P, pair_width * PACK], BF16, align_bytes=64, tag="qf_grouped")
             for i in range(PAIR):
                 regroup(
-                    nc.vector.tensor_copy,
+                    nc.scalar.copy if i == 0 and g < SCALAR_PAIRS else nc.vector.tensor_copy,
                     grouped[:, i * U * PACK : (i + 1) * U * PACK],
                     query_rows[g][:, i, :],
                 )
@@ -159,7 +161,7 @@ def tile_crossattention_pa_t_kernel(tc, query, support, Wk, Wv, out):
                         stop=True,
                     )
                 banks.append(bank)
-            low = soft.tile([P, N_SUP // 2, P], F32, bufs=3)
+            low = soft.tile([P, N_SUP // 2, P], F32, bufs=4)
             nc.scalar.copy(out=low[:], in_=banks[0][:])
             score_banks[b, half] = (low, banks[1])
 
@@ -195,7 +197,7 @@ def tile_crossattention_pa_t_kernel(tc, query, support, Wk, Wv, out):
 
         def add_over_n(b):
             if b % GROUP == 0:
-                denom = soft.tile([P, GROUP, U // P, V], F32)
+                denom = soft.tile([P, GROUP, U // P, V], F32, bufs=2)
                 denoms[b // GROUP] = denom
             denom_ps = turn_psum.tile([P, U // P, V], F32, tag="turn")
             for half in range(U // P):
@@ -206,11 +208,10 @@ def tile_crossattention_pa_t_kernel(tc, query, support, Wk, Wv, out):
             nc.scalar.copy(out=denoms[b // GROUP][:, b % GROUP], in_=denom_ps[:])
 
         def invert(group):
-            logs = soft.tile([P, GROUP, U // P, V], F32)
-            nc.scalar.activation(out=logs[:], in_=denoms[group][:], func=ACT.Ln)
-            recip = soft.tile([P, GROUP, U // P, V], F32)
-            nc.scalar.activation(out=recip[:], in_=logs[:], func=ACT.Exp, scale=-1.0)
-            recips[group] = recip
+            whole = denoms[group][:]
+            nc.scalar.activation(out=whole, in_=whole, func=ACT.Ln)
+            nc.scalar.activation(out=whole, in_=whole, func=ACT.Exp, scale=-1.0)
+            recips[group] = denoms[group]
 
         def turn_back(b):
             recip_ps = turn_psum.tile([P, U], F32, tag="turn")
@@ -223,11 +224,10 @@ def tile_crossattention_pa_t_kernel(tc, query, support, Wk, Wv, out):
             turned[b] = recip_ps
 
         def sum_softmax(b):
-            attn = soft.tile([P, N_FREE, U], F32, bufs=1)
             weight = soft.tile([P, N_FREE], F32)
             for n in range(N_FREE):
                 nc.vector.scalar_tensor_tensor(
-                    out=attn[:, n, :],
+                    out=exps[b][:, n, :],
                     in0=exps[b][:, n, :],
                     scalar=1.0,
                     in1=turned[b][:],
@@ -238,7 +238,7 @@ def tile_crossattention_pa_t_kernel(tc, query, support, Wk, Wv, out):
             weights[b] = weight
 
         def weigh_values(b):
-            weighted = soft.tile([P, N_FREE, DV], F32)
+            weighted = soft.tile([P, N_FREE, DV], F32, bufs=2)
             nc.gpsimd.tensor_tensor(
                 out=weighted[:],
                 in0=val_t[:],
@@ -256,7 +256,7 @@ def tile_crossattention_pa_t_kernel(tc, query, support, Wk, Wv, out):
             )
 
         def store_results(last):
-            result_sb = soft.tile([P, STORE, V], F32)
+            result_sb = soft.tile([P, STORE, V], F32, bufs=2)
             nc.scalar.copy(out=result_sb[:], in_=results[last // STORE][:])
             nc.sync.dma_start(
                 out=out[last - STORE + 1 : last + 1].rearrange("b c v -> c b v"), in_=result_sb[:]
@@ -277,7 +277,7 @@ def tile_crossattention_pa_t_kernel(tc, query, support, Wk, Wv, out):
         sup_scales = keep.tile([P, N_SUP * V], U8, align_bytes=64)
         for n in range(N_SUP):
             regroup(
-                nc.vector.tensor_copy,
+                nc.scalar.copy if n < SCALAR_SUP else nc.vector.tensor_copy,
                 sup_grouped[:, n * V * PACK : (n + 1) * V * PACK],
                 sup_rows[:, n, :],
             )
@@ -342,6 +342,7 @@ def tile_crossattention_pa_t_kernel(tc, query, support, Wk, Wv, out):
                 weigh_values(k - SUM_LAG - 1)
             if 0 <= k - SUM_LAG - 3 and (k - SUM_LAG - 3) % STORE == STORE - 1:
                 store_results(k - SUM_LAG - 3)
+            projection_round(k + FIRST_ROUNDS)
             for half in range(U // P):
                 if k < B:
                     shift_and_exp(k, half)
@@ -357,4 +358,3 @@ def tile_crossattention_pa_t_kernel(tc, query, support, Wk, Wv, out):
                 sum_softmax(k - SUM_LAG)
             if 0 <= k - SUM_LAG + 1 < B:
                 turn_back(k - SUM_LAG + 1)
-            projection_round(k + FIRST_ROUNDS)

@@ -19,11 +19,12 @@ PAIR = 2
 N_PAIRS = B // PAIR
 FIRST_ROUNDS = 3
 STORE = 4
+SUP_LOAD = 2
 GROUP = 4
-SUM_LAG = GROUP + 3
+SUM_LAG = GROUP + 4
 N_FREE = N_SUP - 1
-SCALAR_SUP = 3
 SCALAR_PAIRS = 2
+VECTOR_PAIRS = 1
 RUN = 4
 
 FLOPS = 2 * (B * DK * D * U + N_SUP * DK * D * V + N_SUP * DV * D * V + B * N_SUP * U * V * DK)
@@ -33,22 +34,27 @@ def tile_crossattention_pa_t_kernel(tc, query, support, Wk, Wv, out):
     nc = tc.nc
     with ExitStack() as ctx:
         keep = ctx.enter_context(tc.tile_pool(name="keep", bufs=1))
-        rows_pool = ctx.enter_context(tc.tile_pool(name="rows", bufs=N_PAIRS))
+        rows_pool = ctx.enter_context(tc.tile_pool(name="rows", bufs=N_PAIRS - 1))
         stage = ctx.enter_context(tc.tile_pool(name="stage", bufs=2))
         soft = ctx.enter_context(tc.tile_pool(name="soft", bufs=3))
-        exp_pool = ctx.enter_context(tc.tile_pool(name="exp_pool", bufs=GROUP + 4))
+        exp_pool = ctx.enter_context(tc.tile_pool(name="exp_pool", bufs=GROUP + 5))
         score_psum = ctx.enter_context(tc.psum_pool(name="score_psum", bufs=4))
         turn_psum = ctx.enter_context(tc.psum_pool(name="turn_psum", bufs=3))
         result_psum = ctx.enter_context(tc.psum_pool(name="result_psum", bufs=1))
 
-        wk_rows = keep.tile([P, PACK * D], BF16)
-        nc.sync.dma_start(out=wk_rows[:], in_=Wk.rearrange("(p t) d -> p (t d)", t=PACK))
+        sup_rows = keep.tile([P, N_SUP, PACK * V], BF16)
+        for n in range(0, N_SUP, SUP_LOAD):
+            nc.sync.dma_start(
+                out=sup_rows[:, n : n + SUP_LOAD, :],
+                in_=support[n : n + SUP_LOAD].rearrange("n (p j) h w -> p n (j h w)", j=PACK),
+            )
+        wk_rows = keep.tile([P, PACK, D], BF16)
+        for t in range(PACK):
+            nc.sync.dma_start(
+                out=wk_rows[:, t, :], in_=Wk.rearrange("(p t) d -> p t d", t=PACK)[:, t, :]
+            )
         wv_rows = keep.tile([P, D], BF16)
         nc.sync.dma_start(out=wv_rows[:], in_=Wv)
-        sup_rows = keep.tile([P, N_SUP, PACK * V], BF16)
-        nc.sync.dma_start(
-            out=sup_rows[:], in_=support.rearrange("n (p j) h w -> p n (j h w)", j=PACK)
-        )
         query_rows = []
         for g in range(N_PAIRS):
             q_rows = rows_pool.tile([P, PAIR, PACK * U], BF16)
@@ -79,7 +85,7 @@ def tile_crossattention_pa_t_kernel(tc, query, support, Wk, Wv, out):
                 planes = score_psum.tile([P, 2, P], F32, tag="bank")
                 for e in range(2):
                     nc.tensor.transpose(planes[:, e, :], words[:, t, e, :], ident[:])
-                nc.vector.tensor_copy(
+                nc.scalar.copy(
                     out=grouped_words[:, t], in_=planes[:].rearrange("p e k -> p k e")
                 )
             quantise(codes, scales, grouped)
@@ -130,9 +136,9 @@ def tile_crossattention_pa_t_kernel(tc, query, support, Wk, Wv, out):
         def project_queries(g):
             grouped = stage.tile([P, pair_width * PACK], BF16, align_bytes=64, tag="q_grouped")
             codes, scales = qf_operands[g]
-            project_with_wk(
-                turn_psum, "turn", codes, scales, grouped, pair_width // P, [nc.scalar.copy]
-            )
+            late = g >= N_PAIRS - VECTOR_PAIRS
+            copies = [nc.vector.tensor_copy if late else nc.scalar.copy]
+            project_with_wk(turn_psum, "turn", codes, scales, grouped, pair_width // P, copies)
             q_grouped[g] = grouped
 
         def quantise_projected(g):
@@ -170,11 +176,15 @@ def tile_crossattention_pa_t_kernel(tc, query, support, Wk, Wv, out):
                 expd = exp_pool.tile([P, N_SUP, U], F32)
                 exps[b] = expd
             low, high = score_banks[b, half]
-            top4 = soft.tile([P, N_SUP // 2, P], F32)
-            nc.vector.tensor_max(out=top4[:], in0=high[:], in1=low[:])
+            top4 = soft.tile([P, 2, P, 2], F32)
+            nc.vector.tensor_max(
+                out=top4[:],
+                in0=high[:].rearrange("p (a b) u -> p a u b", b=2),
+                in1=low[:].rearrange("p (a b) u -> p a u b", b=2),
+            )
             top = soft.tile([P, P], F32)
             nc.vector.reduce_max(
-                out=top[:], in_=top4[:].rearrange("p n u -> p u n"), axis=mybir.AxisListType.X
+                out=top[:], in_=top4[:].rearrange("p a u b -> p u a b"), axis=mybir.AxisListType.XY
             )
             mine = exps[b][:, :, half * P : (half + 1) * P]
             top_of_each = top[:].unsqueeze(1).to_broadcast([P, N_SUP // 2, P])
@@ -239,7 +249,8 @@ def tile_crossattention_pa_t_kernel(tc, query, support, Wk, Wv, out):
 
         def weigh_values(b):
             weighted = soft.tile([P, N_FREE, DV], F32, bufs=2)
-            nc.gpsimd.tensor_tensor(
+            engine = nc.vector if b == B - 1 else nc.gpsimd
+            engine.tensor_tensor(
                 out=weighted[:],
                 in0=val_t[:],
                 in1=weights[b][:].unsqueeze(2).to_broadcast([P, N_FREE, DV]),
@@ -255,17 +266,18 @@ def tile_crossattention_pa_t_kernel(tc, query, support, Wk, Wv, out):
                 results[b // STORE][:, b % STORE, :], [products[b][:, n, :] for n in range(N_FREE)] + [base[:]]
             )
 
-        def store_results(last):
-            result_sb = soft.tile([P, STORE, V], F32, bufs=2)
-            nc.scalar.copy(out=result_sb[:], in_=results[last // STORE][:])
+        def store_results(first, end):
+            result_sb = soft.tile([P, end - first, V], F32, bufs=2)
+            places = slice(first % STORE, first % STORE + end - first)
+            nc.scalar.copy(out=result_sb[:], in_=results[first // STORE][:, places, :])
             nc.sync.dma_start(
-                out=out[last - STORE + 1 : last + 1].rearrange("b c v -> c b v"), in_=result_sb[:]
+                out=out[first:end].rearrange("b c v -> c b v"), in_=result_sb[:]
             )
 
         wk_grouped = keep.tile([P, PACK * DK], BF16, align_bytes=64)
         wk_codes = keep.tile([P, DK], U32, align_bytes=64)
         wk_scales = keep.tile([P, DK], U8, align_bytes=64)
-        weight_to_codes(wk_rows[:], PACK, wk_grouped[:], wk_codes[:], wk_scales[:])
+        weight_to_codes(wk_rows[:].rearrange("p t d -> p (t d)"), PACK, wk_grouped[:], wk_codes[:], wk_scales[:])
         wv_grouped = keep.tile([P, PACK * DV], BF16, align_bytes=64)
         wv_codes = keep.tile([P, DV], U32, align_bytes=64)
         wv_scales = keep.tile([P, DV], U8, align_bytes=64)
@@ -277,7 +289,7 @@ def tile_crossattention_pa_t_kernel(tc, query, support, Wk, Wv, out):
         sup_scales = keep.tile([P, N_SUP * V], U8, align_bytes=64)
         for n in range(N_SUP):
             regroup(
-                nc.scalar.copy if n < SCALAR_SUP else nc.vector.tensor_copy,
+                nc.vector.tensor_copy,
                 sup_grouped[:, n * V * PACK : (n + 1) * V * PACK],
                 sup_rows[:, n, :],
             )
@@ -297,10 +309,8 @@ def tile_crossattention_pa_t_kernel(tc, query, support, Wk, Wv, out):
         )
         quantise(key_codes[:], key_scales[:], key_grouped[:])
 
-        val_t = keep.tile([P, N_FREE, DV], F32)
-        val_last = keep.tile([P, DV], F32)
-        base = keep.tile([P, DV], F32)
-        for half in reversed(range(N_SUP // PACK)):
+        val_sb = keep.tile([P, N_SUP, DV], F32)
+        for half in range(N_SUP // PACK):
             val_ps = score_psum.tile([P, PACK, DV], F32, tag="bank")
             for i in range(PACK):
                 cols = slice((half * PACK + i) * V, (half * PACK + i + 1) * V)
@@ -313,15 +323,16 @@ def tile_crossattention_pa_t_kernel(tc, query, support, Wk, Wv, out):
                     start=True,
                     stop=True,
                 )
-            if half == N_SUP // PACK - 1:
-                nc.scalar.copy(out=val_last[:], in_=val_ps[:, PACK - 1, :])
-                nc.scalar.mul(out=base[:], in_=val_last[:], mul=float(U))
-            n_here = min(N_FREE - half * PACK, PACK)
-            nc.vector.tensor_sub(
-                out=val_t[:, half * PACK : half * PACK + n_here, :],
-                in0=val_ps[:, 0:n_here, :],
-                in1=val_last[:].unsqueeze(1).to_broadcast([P, n_here, DV]),
-            )
+            nc.scalar.copy(out=val_sb[:, half * PACK : (half + 1) * PACK, :], in_=val_ps[:])
+        base = keep.tile([P, DV], F32)
+        nc.scalar.mul(out=base[:], in_=val_sb[:, N_FREE, :], mul=float(U))
+        val_t = keep.tile([P, N_FREE, DV], F32)
+        nc.gpsimd.tensor_tensor(
+            out=val_t[:],
+            in0=val_sb[:, 0:N_FREE, :],
+            in1=val_sb[:, N_FREE : N_FREE + 1, :].to_broadcast([P, N_FREE, DV]),
+            op=ALU.subtract,
+        )
 
         def projection_round(g):
             if g < N_PAIRS:
@@ -340,8 +351,13 @@ def tile_crossattention_pa_t_kernel(tc, query, support, Wk, Wv, out):
         for k in range(B + SUM_LAG + 3):
             if 0 <= k - SUM_LAG - 1 < B:
                 weigh_values(k - SUM_LAG - 1)
-            if 0 <= k - SUM_LAG - 3 and (k - SUM_LAG - 3) % STORE == STORE - 1:
-                store_results(k - SUM_LAG - 3)
+            done = k - SUM_LAG - 2
+            if 0 < done < B and done % STORE == 0:
+                store_results(done - STORE, done)
+            if done == B - 1:
+                store_results(B - STORE, B - 1)
+            if done == B:
+                store_results(B - 1, B)
             projection_round(k + FIRST_ROUNDS)
             for half in range(U // P):
                 if k < B:

@@ -21,6 +21,7 @@ FIRST_ROUNDS = 3
 STORE = 4
 SUP_LOAD = 2
 GROUP = 4
+COPY_AHEAD = 100
 SUM_LAG = GROUP + 4
 N_FREE = N_SUP - 1
 SCALAR_PAIRS = 2
@@ -168,7 +169,8 @@ def tile_crossattention_pa_t_kernel(tc, query, support, Wk, Wv, out):
                     )
                 banks.append(bank)
             low = soft.tile([P, N_SUP // 2, P], F32, bufs=4)
-            nc.scalar.copy(out=low[:], in_=banks[0][:])
+            with tc.high_priority(offset=COPY_AHEAD):
+                nc.scalar.copy(out=low[:], in_=banks[0][:])
             score_banks[b, half] = (low, banks[1])
 
         def shift_and_exp(b, half):

@@ -71,9 +71,10 @@ def tile_crossattention_pa_t_kernel(tc, query, support, Wk, Wv, out):
         make_identity(nc, ident[:])
 
         def regroup(engine_copy, grouped, rows):
+            images = rows.shape[1]
             engine_copy(
-                out=grouped.rearrange("p (c r j) -> p c j r", r=RUN, j=PACK),
-                in_=rows.rearrange("p (j c r) -> p c j r", j=PACK, r=RUN),
+                out=grouped.rearrange("p (i c r j) -> p i c j r", i=images, r=RUN, j=PACK),
+                in_=rows.rearrange("p i (j c r) -> p i c j r", j=PACK, r=RUN),
             )
 
         def quantise(codes, scales, grouped):
@@ -120,12 +121,11 @@ def tile_crossattention_pa_t_kernel(tc, query, support, Wk, Wv, out):
 
         def regroup_queries(g):
             grouped = stage.tile([P, pair_width * PACK], BF16, align_bytes=64, tag="qf_grouped")
-            for i in range(PAIR):
-                regroup(
-                    nc.scalar.copy if i == 0 and g < SCALAR_PAIRS else nc.vector.tensor_copy,
-                    grouped[:, i * U * PACK : (i + 1) * U * PACK],
-                    query_rows[g][:, i, :],
-                )
+            by_scalar = 1 if g < SCALAR_PAIRS else 0
+            split = by_scalar * U * PACK
+            if by_scalar:
+                regroup(nc.scalar.copy, grouped[:, 0:split], query_rows[g][:, 0:by_scalar, :])
+            regroup(nc.vector.tensor_copy, grouped[:, split:], query_rows[g][:, by_scalar:, :])
             qf_grouped[g] = grouped
 
         def quantise_queries(g):
@@ -289,11 +289,11 @@ def tile_crossattention_pa_t_kernel(tc, query, support, Wk, Wv, out):
         sup_grouped = keep.tile([P, N_SUP * V * PACK], BF16, align_bytes=64)
         sup_codes = keep.tile([P, N_SUP * V], U32, align_bytes=64)
         sup_scales = keep.tile([P, N_SUP * V], U8, align_bytes=64)
-        for n in range(N_SUP):
+        for n in range(0, N_SUP, SUP_LOAD):
             regroup(
                 nc.vector.tensor_copy,
-                sup_grouped[:, n * V * PACK : (n + 1) * V * PACK],
-                sup_rows[:, n, :],
+                sup_grouped[:, n * V * PACK : (n + SUP_LOAD) * V * PACK],
+                sup_rows[:, n : n + SUP_LOAD, :],
             )
         quantise(sup_codes[:], sup_scales[:], sup_grouped[:])
 

@@ -366,10 +366,10 @@ def tile_crossattention_pa_t_kernel(tc, query, support, Wk, Wv, out):
                     shift_and_exp(k, half)
                 if k + 1 < B:
                     scores(k + 1, half)
-            if 0 <= k - 1 < B:
-                add_over_n(k - 1)
-                if k % GROUP == 0:
-                    invert((k - 1) // GROUP)
+            if 0 <= k - 2 < B:
+                add_over_n(k - 2)
+                if (k - 1) % GROUP == 0:
+                    invert((k - 2) // GROUP)
             if 0 <= k - SUM_LAG - 2 < B:
                 combine(k - SUM_LAG - 2)
             if 0 <= k - SUM_LAG < B:

import math
from contextlib import ExitStack

import concourse.mybir as mybir
from concourse.masks import make_identity

F32 = mybir.dt.float32
BF16 = mybir.dt.bfloat16
U32 = mybir.dt.uint32
U8 = mybir.dt.uint8
FP8X4 = mybir.dt.float8_e4m3fn_x4
ACT = mybir.ActivationFunctionType
ALU = mybir.AluOpType

P = 128
PACK = 4
B, N_SUP, D, DK, DV, U, V = 16, 8, 512, 512, 128, 256, 128
PAIR = 2
N_PAIRS = B // PAIR
FIRST_ROUNDS = 3
STORE = 4
SUP_LOAD = 2
GROUP = 4
COPY_AHEAD = 100
SUM_LAG = GROUP + 4
N_FREE = N_SUP - 1
SCALAR_PAIRS = 2
VECTOR_PAIRS = 1
RUN = 4

FLOPS = 2 * (B * DK * D * U + N_SUP * DK * D * V + N_SUP * DV * D * V + B * N_SUP * U * V * DK)


def tile_crossattention_pa_t_kernel(tc, query, support, Wk, Wv, out):
    nc = tc.nc
    with ExitStack() as ctx:
        keep = ctx.enter_context(tc.tile_pool(name="keep", bufs=1))
        rows_pool = ctx.enter_context(tc.tile_pool(name="rows", bufs=N_PAIRS - 1))
        stage = ctx.enter_context(tc.tile_pool(name="stage", bufs=2))
        soft = ctx.enter_context(tc.tile_pool(name="soft", bufs=3))
        exp_pool = ctx.enter_context(tc.tile_pool(name="exp_pool", bufs=GROUP + 5))
        score_psum = ctx.enter_context(tc.psum_pool(name="score_psum", bufs=4))
        turn_psum = ctx.enter_context(tc.psum_pool(name="turn_psum", bufs=3))
        result_psum = ctx.enter_context(tc.psum_pool(name="result_psum", bufs=1))

        sup_rows = keep.tile([P, N_SUP, PACK * V], BF16)
        for n in range(0, N_SUP, SUP_LOAD):
            nc.sync.dma_start(
                out=sup_rows[:, n : n + SUP_LOAD, :],
                in_=support[n : n + SUP_LOAD].rearrange("n (p j) h w -> p n (j h w)", j=PACK),
            )
        wk_rows = keep.tile([P, PACK, D], BF16)
        for t in range(PACK):
            nc.sync.dma_start(
                out=wk_rows[:, t, :], in_=Wk.rearrange("(p t) d -> p t d", t=PACK)[:, t, :]
            )
        wv_rows = keep.tile([P, D], BF16)
        nc.sync.dma_start(out=wv_rows[:], in_=Wv)
        query_rows = []
        for g in range(N_PAIRS):
            q_rows = rows_pool.tile([P, PAIR, PACK * U], BF16)
            nc.sync.dma_start(
                out=q_rows[:],
                in_=query[g * PAIR : (g + 1) * PAIR].rearrange(
                    "b (p j) h w -> p b (j h w)", j=PACK
                ),
            )
            query_rows.append(q_rows)

        ident = keep.tile([P, P], F32)
        make_identity(nc, ident[:])

        def regroup(engine_copy, grouped, rows):
            images = rows.shape[1]
            engine_copy(
                out=grouped.rearrange("p (i c r j) -> p i c j r", i=images, r=RUN, j=PACK),
                in_=rows.rearrange("p i (j c r) -> p i c j r", j=PACK, r=RUN),
            )

        def quantise(codes, scales, grouped):
            nc.vector.quantize_mx(out=codes.bitcast(FP8X4), scales=scales, in_=grouped)

        def weight_to_codes(rows, n_chunks, grouped, codes, scales):
            words = rows.bitcast(F32).rearrange("p (t w e) -> p t e w", t=n_chunks, e=2)
            grouped_words = grouped.bitcast(F32).rearrange("p (t k e) -> p t k e", t=n_chunks, e=2)
            for t in range(n_chunks):
                planes = score_psum.tile([P, 2, P], F32, tag="bank")
                for e in range(2):
                    nc.tensor.transpose(planes[:, e, :], words[:, t, e, :], ident[:])
                nc.scalar.copy(
                    out=grouped_words[:, t], in_=planes[:].rearrange("p e k -> p k e")
                )
            quantise(codes, scales, grouped)

        def project_with_wk(psum, tag, x_codes, x_scales, grouped, n_blocks, copies):
            for blk in range(n_blocks):
                cols = slice(blk * P, (blk + 1) * P)
                prod = psum.tile([P, PACK, P], F32, tag=tag)
                for j in range(PACK):
                    chunk = slice(j * P, (j + 1) * P)
                    nc.tensor.matmul_mx(
                        out=prod[:, j, :],
                        lhsT=wk_codes[:, chunk].bitcast(FP8X4),
                        lhsT_scale=wk_scales[:, chunk],
                        rhs=x_codes[:, cols].bitcast(FP8X4),
                        rhs_scale=x_scales[:, cols],
                        start=True,
                        stop=True,
                    )
                copies[blk % len(copies)](
                    out=grouped[:, blk * P * PACK : (blk + 1) * P * PACK].rearrange(
                        "p (c j) -> p c j", j=PACK
                    ),
                    in_=prod[:].rearrange("p j c -> p c j"),
                )

        pair_width = PAIR * U
        qf_grouped, qf_operands, q_grouped = {}, {}, {}
        q_codes = keep.tile([P, B * U], U32, align_bytes=64)
        q_scales = keep.tile([P, B * U], U8, align_bytes=64)

        def regroup_queries(g):
            grouped = stage.tile([P, pair_width * PACK], BF16, align_bytes=64, tag="qf_grouped")
            by_scalar = 1 if g < SCALAR_PAIRS else 0
            split = by_scalar * U * PACK
            if by_scalar:
                regroup(nc.scalar.copy, grouped[:, 0:split], query_rows[g][:, 0:by_scalar, :])
            regroup(nc.vector.tensor_copy, grouped[:, split:], query_rows[g][:, by_scalar:, :])
            qf_grouped[g] = grouped

        def quantise_queries(g):
            codes = stage.tile([P, pair_width], U32, align_bytes=64, tag="qf_codes")
            scales = stage.tile([P, pair_width], U8, align_bytes=64, tag="qf_scales")
            quantise(codes[:], scales[:], qf_grouped[g][:])
            qf_operands[g] = (codes, scales)

        def project_queries(g):
            grouped = stage.tile([P, pair_width * PACK], BF16, align_bytes=64, tag="q_grouped")
            codes, scales = qf_operands[g]
            late = g >= N_PAIRS - VECTOR_PAIRS
            copies = [nc.vector.tensor_copy if late else nc.scalar.copy]
            project_with_wk(turn_psum, "turn", codes, scales, grouped, pair_width // P, copies)
            q_grouped[g] = grouped

        def quantise_projected(g):
            cols = slice(g * pair_width, (g + 1) * pair_width)
            quantise(q_codes[:, cols], q_scales[:, cols], q_grouped[g][:])

        score_banks, exps, denoms, recips, turned, weights, products, results = (
            {}, {}, {}, {}, {}, {}, {}, {}
        )

        def scores(b, half):
            u_cols = slice(b * U + half * P, b * U + (half + 1) * P)
            banks = []
            for j in range(2):
                bank = score_psum.tile([P, N_SUP // 2, P], F32, tag="bank")
                for i in range(N_SUP // 2):
                    n = j * (N_SUP // 2) + i
                    v_cols = slice(n * V, (n + 1) * V)
                    nc.tensor.matmul_mx(
                        out=bank[:, i, :],
                        lhsT=key_codes[:, v_cols].bitcast(FP8X4),
                        lhsT_scale=key_scales[:, v_cols],
                        rhs=q_codes[:, u_cols].bitcast(FP8X4),
                        rhs_scale=q_scales[:, u_cols],
                        start=True,
                        stop=True,
                    )
                banks.append(bank)
            low = soft.tile([P, N_SUP // 2, P], F32, bufs=4)
            with tc.high_priority(offset=COPY_AHEAD):
                nc.scalar.copy(out=low[:], in_=banks[0][:])
            score_banks[b, half] = (low, banks[1])

        def shift_and_exp(b, half):
            if half == 0:
                expd = exp_pool.tile([P, N_SUP, U], F32)
                exps[b] = expd
            low, high = score_banks[b, half]
            top4 = soft.tile([P, 2, P, 2], F32)
            nc.vector.tensor_max(
                out=top4[:],
                in0=high[:].rearrange("p (a b) u -> p a u b", b=2),
                in1=low[:].rearrange("p (a b) u -> p a u b", b=2),
            )
            top = soft.tile([P, P], F32)
            nc.vector.reduce_max(
                out=top[:], in_=top4[:].rearrange("p a u b -> p u a b"), axis=mybir.AxisListType.XY
            )
            mine = exps[b][:, :, half * P : (half + 1) * P]
            top_of_each = top[:].unsqueeze(1).to_broadcast([P, N_SUP // 2, P])
            nc.gpsimd.tensor_tensor(
                out=mine[:, 0 : N_SUP // 2, :], in0=low[:], in1=top_of_each, op=ALU.subtract
            )
            nc.vector.tensor_sub(out=mine[:, N_SUP // 2 : N_SUP, :], in0=high[:], in1=top_of_each)
            nc.scalar.activation(out=mine, in_=mine, func=ACT.Exp, scale=1.0 / math.sqrt(DK))

        def add_transposed(out_ps, terms):
            for i, term in enumerate(terms):
                nc.tensor.matmul(
                    out=out_ps,
                    lhsT=term,
                    rhs=ident[:],
                    is_transpose=True,
                    start=(i == 0),
                    stop=(i == len(terms) - 1),
                )

        def add_over_n(b):
            if b % GROUP == 0:
                denom = soft.tile([P, GROUP, U // P, V], F32, bufs=2)
                denoms[b // GROUP] = denom
            denom_ps = turn_psum.tile([P, U // P, V], F32, tag="turn")
            for half in range(U // P):
                add_transposed(
                    denom_ps[:, half, :],
                    [exps[b][:, n, half * P : (half + 1) * P] for n in range(N_SUP)],
                )
            nc.scalar.copy(out=denoms[b // GROUP][:, b % GROUP], in_=denom_ps[:])

        def invert(group):
            whole = denoms[group][:]
            nc.scalar.activation(out=whole, in_=whole, func=ACT.Ln)
            nc.scalar.activation(out=whole, in_=whole, func=ACT.Exp, scale=-1.0)
            recips[group] = denoms[group]

        def turn_back(b):
            recip_ps = turn_psum.tile([P, U], F32, tag="turn")
            for half in range(U // P):
                nc.tensor.transpose(
                    recip_ps[:, half * P : (half + 1) * P],
                    recips[b // GROUP][:, b % GROUP, half, :],
                    ident[:],
                )
            turned[b] = recip_ps

        def sum_softmax(b):
            weight = soft.tile([P, N_FREE], F32)
            for n in range(N_FREE):
                nc.vector.scalar_tensor_tensor(
                    out=exps[b][:, n, :],
                    in0=exps[b][:, n, :],
                    scalar=1.0,
                    in1=turned[b][:],
                    op0=ALU.mult,
                    op1=ALU.mult,
                    accum_out=weight[:, n : n + 1],
                )
            weights[b] = weight

        def weigh_values(b):
            weighted = soft.tile([P, N_FREE, DV], F32, bufs=2)
            engine = nc.vector if b == B - 1 else nc.gpsimd
            engine.tensor_tensor(
                out=weighted[:],
                in0=val_t[:],
                in1=weights[b][:].unsqueeze(2).to_broadcast([P, N_FREE, DV]),
                op=ALU.mult,
            )
            products[b] = weighted

        def combine(b):
            if b % STORE == 0:
                result_ps = result_psum.tile([P, STORE, V], F32)
                results[b // STORE] = result_ps
            add_transposed(
                results[b // STORE][:, b % STORE, :], [products[b][:, n, :] for n in range(N_FREE)] + [base[:]]
            )

        def store_results(first, end):
            result_sb = soft.tile([P, end - first, V], F32, bufs=2)
            places = slice(first % STORE, first % STORE + end - first)
            nc.scalar.copy(out=result_sb[:], in_=results[first // STORE][:, places, :])
            nc.sync.dma_start(
                out=out[first:end].rearrange("b c v -> c b v"), in_=result_sb[:]
            )

        wk_grouped = keep.tile([P, PACK * DK], BF16, align_bytes=64)
        wk_codes = keep.tile([P, DK], U32, align_bytes=64)
        wk_scales = keep.tile([P, DK], U8, align_bytes=64)
        weight_to_codes(wk_rows[:].rearrange("p t d -> p (t d)"), PACK, wk_grouped[:], wk_codes[:], wk_scales[:])
        wv_grouped = keep.tile([P, PACK * DV], BF16, align_bytes=64)
        wv_codes = keep.tile([P, DV], U32, align_bytes=64)
        wv_scales = keep.tile([P, DV], U8, align_bytes=64)
        weight_to_codes(wv_rows[:], 1, wv_grouped[:], wv_codes[:], wv_scales[:])


        sup_grouped = keep.tile([P, N_SUP * V * PACK], BF16, align_bytes=64)
        sup_codes = keep.tile([P, N_SUP * V], U32, align_bytes=64)
        sup_scales = keep.tile([P, N_SUP * V], U8, align_bytes=64)
        for n in range(0, N_SUP, SUP_LOAD):
            regroup(
                nc.vector.tensor_copy,
                sup_grouped[:, n * V * PACK : (n + SUP_LOAD) * V * PACK],
                sup_rows[:, n : n + SUP_LOAD, :],
            )
        quantise(sup_codes[:], sup_scales[:], sup_grouped[:])

        key_grouped = keep.tile([P, N_SUP * V * PACK], BF16, align_bytes=64)
        key_codes = keep.tile([P, N_SUP * V], U32, align_bytes=64)
        key_scales = keep.tile([P, N_SUP * V], U8, align_bytes=64)
        project_with_wk(
            score_psum,
            "bank",
            sup_codes,
            sup_scales,
            key_grouped,
            N_SUP,
            [nc.scalar.copy, nc.vector.tensor_copy],
        )
        quantise(key_codes[:], key_scales[:], key_grouped[:])

        val_sb = keep.tile([P, N_SUP, DV], F32)
        for half in range(N_SUP // PACK):
            val_ps = score_psum.tile([P, PACK, DV], F32, tag="bank")
            for i in range(PACK):
                cols = slice((half * PACK + i) * V, (half * PACK + i + 1) * V)
                nc.tensor.matmul_mx(
                    out=val_ps[:, i, :],
                    lhsT=sup_codes[:, cols].bitcast(FP8X4),
                    lhsT_scale=sup_scales[:, cols],
                    rhs=wv_codes[:].bitcast(FP8X4),
                    rhs_scale=wv_scales[:],
                    start=True,
                    stop=True,
                )
            nc.scalar.copy(out=val_sb[:, half * PACK : (half + 1) * PACK, :], in_=val_ps[:])
        base = keep.tile([P, DV], F32)
        nc.scalar.mul(out=base[:], in_=val_sb[:, N_FREE, :], mul=float(U))
        val_t = keep.tile([P, N_FREE, DV], F32)
        nc.gpsimd.tensor_tensor(
            out=val_t[:],
            in0=val_sb[:, 0:N_FREE, :],
            in1=val_sb[:, N_FREE : N_FREE + 1, :].to_broadcast([P, N_FREE, DV]),
            op=ALU.subtract,
        )

        def projection_round(g):
            if g < N_PAIRS:
                regroup_queries(g)
            if 0 <= g - 1 < N_PAIRS:
                quantise_queries(g - 1)
                project_queries(g - 1)
            if 0 <= g - 2 < N_PAIRS:
                quantise_projected(g - 2)

        for g in range(FIRST_ROUNDS):
            projection_round(g)

        for half in range(U // P):
            scores(0, half)
        for k in range(B + SUM_LAG + 3):
            if 0 <= k - SUM_LAG - 1 < B:
                weigh_values(k - SUM_LAG - 1)
            done = k - SUM_LAG - 2
            if 0 < done < B and done % STORE == 0:
                store_results(done - STORE, done)
            if done == B - 1:
                store_results(B - STORE, B - 1)
            if done == B:
                store_results(B - 1, B)
            projection_round(k + FIRST_ROUNDS)
            for half in range(U // P):
                if k < B:
                    shift_and_exp(k, half)
                if k + 1 < B:
                    scores(k + 1, half)
            if 0 <= k - 2 < B:
                add_over_n(k - 2)
                if (k - 1) % GROUP == 0:
                    invert((k - 2) // GROUP)
            if 0 <= k - SUM_LAG - 2 < B:
                combine(k - SUM_LAG - 2)
            if 0 <= k - SUM_LAG < B:
                sum_softmax(k - SUM_LAG)
            if 0 <= k - SUM_LAG + 1 < B:
                turn_back(k - SUM_LAG + 1)
